import numpy as np
import ml_dtypes


def mxq(x, axis, fmt="e4m3"):
    dtype, down = {"e4m3": (ml_dtypes.float8_e4m3fn, 7), "e5m2": (ml_dtypes.float8_e5m2, 14)}[fmt]
    v = np.moveaxis(np.asarray(x, np.float32).astype(ml_dtypes.bfloat16).astype(np.float64), axis, -1)
    blocks = v.reshape(v.shape[:-1] + (-1, 32))
    amax = np.abs(blocks).max(-1, keepdims=True)
    byte = np.maximum(np.where(amax > 0, np.frexp(amax)[1] - 1 + 127, 0) - down, 1)
    scale = np.exp2(byte - 127.0)
    codes = (blocks / scale).astype(np.float32).astype(dtype).astype(np.float64)
    return np.moveaxis((codes * scale).reshape(v.shape), -1, axis)


WIDE = False


def mx_kscale(k):
    if not WIDE:
        return np.ones(k)
    levels = np.array([10, -10, 5, -5, 0])
    a = np.random.permutation(np.resize(levels, k // 512 * 4)).reshape(k // 512, 4)
    idx = np.arange(k)
    return np.exp2(a[idx // 512, idx % 128 // 32])


BF16 = ml_dtypes.bfloat16


def bf(x):
    return np.asarray(x, np.float32).astype(BF16)


def f64(x):
    return np.asarray(x).astype(np.float64)


B, T, D = 8, 512, 256
GAMMA = 0.5
EPS = 1e-06
REL_THRESH = 1e-09


def setup_inputs():
    s = mx_kscale(T)
    a = np.random.uniform(0.0, 1.0, (B, T, T))
    a = 0.5 * (a + a.transpose(0, 2, 1))
    k = np.random.standard_normal((B, T, D)) * np.sqrt(T)
    return {"A_rel": bf(a * s), "k_seq": bf(k * np.mean(s) / s[:, None])}


def reference(A_rel, k_seq):
    A = f64(A_rel)
    deg = np.sum(A, axis=-1) + EPS
    d_inv_sqrt = 1.0 / np.sqrt(deg)
    W = A * d_inv_sqrt[:, :, None] * d_inv_sqrt[:, None, :]
    n = A.shape[1]
    tril = np.tril(np.ones((n, n)))
    W_causal = W * tril
    a = mxq(W_causal, 2, "e4m3") @ mxq(f64(k_seq), 1, "e4m3")
    has_relation = np.max(np.abs(W) * tril, axis=-1) > REL_THRESH
    a_scaled = a * np.sqrt(GAMMA)
    out = a_scaled * has_relation[:, :, None].astype(np.float64)
    return out

@@ -1,0 +1,189 @@
+import math
+from contextlib import ExitStack
+
+import concourse.mybir as mybir
+from concourse.masks import make_identity
+
+F32 = mybir.dt.float32
+BF16 = mybir.dt.bfloat16
+U32 = mybir.dt.uint32
+U8 = mybir.dt.uint8
+I32 = mybir.dt.int32
+FP8X4 = mybir.dt.float8_e4m3fn_x4
+ALU = mybir.AluOpType
+ACT = mybir.ActivationFunctionType
+AX = mybir.AxisListType
+
+B, T, D = 8, 512, 256
+P = 128
+NT = T // P
+GAMMA = 0.5
+EPS = 1e-06
+REL_THRESH = 1e-09
+FLOPS = 2 * B * T * T * D
+NGW = 3
+
+
+def tile_symbolicpenaltytracker_kernel(tc, A_rel, k_seq, out):
+    nc = tc.nc
+    with ExitStack() as ctx:
+        const = ctx.enter_context(tc.tile_pool(name="const", bufs=1))
+        resid = ctx.enter_context(tc.tile_pool(name="resid", bufs=1))
+        small = ctx.enter_context(tc.tile_pool(name="small", bufs=4))
+        work = ctx.enter_context(tc.tile_pool(name="work", bufs=3))
+        ps_d = ctx.enter_context(tc.psum_pool(name="ps_d", bufs=2))
+        ps_t = ctx.enter_context(tc.psum_pool(name="ps_t", bufs=1))
+        ps_x = ctx.enter_context(tc.psum_pool(name="ps_x", bufs=1))
+        ps_o = ctx.enter_context(tc.psum_pool(name="ps_o", bufs=2))
+
+        a_sb = []
+        k_sb = []
+        for b in range(B):
+            at = resid.tile([P, NT * 640], BF16, name="a%d" % b)
+            kt = resid.tile([P, NT, D], BF16, name="k%d" % b)
+            nc.sync.dma_start(
+                out=at[:, 0 : NT * T].rearrange("p (i s) -> p i s", s=T),
+                in_=A_rel[b].rearrange("(i p) s -> p i s", p=P),
+            )
+            nc.sync.dma_start(out=kt[:], in_=k_seq[b].rearrange("(u p) d -> p u d", p=P))
+            a_sb.append(at)
+            k_sb.append(kt)
+
+        warm = const.tile([P, 1], F32, name="warm")
+        nc.vector.memset(warm[:], 1.0)
+        nc.scalar.activation(out=warm[:], in_=warm[:], func=ACT.Sqrt)
+
+        ident = const.tile([P, P], F32, name="ident")
+        make_identity(nc, ident[:])
+        identb = const.tile([P, P], BF16, name="identb")
+        make_identity(nc, identb[:])
+        trilf = const.tile([P, P], F32, name="trilf")
+        nc.gpsimd.memset(trilf[:], 1.0)
+        nc.gpsimd.affine_select(
+            out=trilf[:], in_=trilf[:], compare_op=ALU.is_ge, fill=0.0, base=0,
+            pattern=[[-1, P]], channel_multiplier=1,
+        )
+        trilb = const.tile([P, P], BF16, name="trilb")
+        nc.vector.tensor_copy(out=trilb[:], in_=trilf[:])
+
+        gws = []
+        for j in range(NGW):
+            g = const.tile([P, NT * P * 4], BF16, name="gw%d" % j, align_bytes=64)
+            nc.vector.memset(g[:], 0.0)
+            gws.append(g)
+
+        st = {}
+
+        def kprep(b):
+            kg = work.tile([P, D * 4], BF16, name="kg", align_bytes=64)
+            nc.vector.tensor_copy(
+                out=kg[:].rearrange("p (c i t) -> p c t i", i=4, t=4),
+                in_=k_sb[b][:].rearrange("p t (c i) -> p c t i", i=4),
+            )
+            kc = resid.tile([P, D], U32, name="kc%d" % b, align_bytes=64)
+            ks = resid.tile([P, D], U8, name="ks%d" % b, align_bytes=64)
+            nc.vector.quantize_mx(out=kc[:].bitcast(FP8X4), scales=ks[:], in_=kg[:])
+            st[("k", b)] = (kc, ks)
+
+        def s1(b):
+            a3 = a_sb[b][:, 0 : NT * T].rearrange("p (i s) -> p i s", s=T)
+            deg = small.tile([P, NT], F32, name="deg")
+            for i in range(NT):
+                junk = work.tile([P, T], BF16, name="junk")
+                nc.scalar.activation(out=junk[:], in_=a3[:, i, :], func=ACT.Copy, accum_out=deg[:, i : i + 1])
+            sd = small.tile([P, NT], F32, name="sd")
+            nc.scalar.activation(out=sd[:], in_=deg[:], func=ACT.Sqrt, bias=EPS)
+            thr = small.tile([P, NT], F32, name="thr")
+            nc.scalar.mul(out=thr[:], in_=sd[:], mul=REL_THRESH)
+            dis = small.tile([P, NT], F32, name="dis")
+            nc.vector.reciprocal(out=dis[:], in_=sd[:])
+            adiag = a_sb[b][:].rearrange("p (i x) -> p i x", x=640)[:, :, 0:P]
+            nc.gpsimd.tensor_tensor(
+                out=adiag, in0=adiag, in1=trilb[:].unsqueeze(1).to_broadcast([P, NT, P]), op=ALU.mult
+            )
+            aabs = work.tile([P, NT * T], BF16, name="aabs")
+            nc.vector.tensor_single_scalar(
+                out=aabs[:].bitcast(I32), in_=a_sb[b][:, 0 : NT * T].bitcast(I32), scalar=0x7FFF7FFF, op=ALU.bitwise_and
+            )
+            dps = ps_d.tile([P, T], F32, name="dps")
+            tps = ps_t.tile([P, T], F32, name="tps")
+            for dst, src in ((dps, dis), (tps, thr)):
+                for m in range(NT):
+                    nc.tensor.transpose(
+                        out=dst[:, m * P : (m + 1) * P],
+                        in_=src[:, m : m + 1].to_broadcast([P, P]),
+                        identity=ident[:],
+                    )
+            st[("d", b)] = (dis, dps, tps, aabs)
+
+        def s2a(b):
+            a3 = a_sb[b][:, 0 : NT * T].rearrange("p (i s) -> p i s", s=T)
+            dis, dps, tps, aabs = st[("d", b)]
+            ab3 = aabs[:].rearrange("p (i s) -> p i s", s=T)
+            wbf = work.tile([P, NT, T], BF16, name="wbf")
+            cnt = small.tile([P, NT], F32, name="cnt")
+            gw = gws[b % NGW]
+            gw4 = gw[:].rearrange("p (i t u) -> p i t u", t=P, u=4)
+            xa = ps_x.tile([P, 8, P], BF16, name="xa", bufs=2)
+            xb = ps_x.tile([P, 2, P], BF16, name="xb", bufs=1)
+            place = {3: (xa, 0), 2: (xa, 4), 0: (xa, 7), 1: (xb, 0)}
+            for i in (3, 2, 1, 0):
+                n = (i + 1) * P
+                nc.vector.scalar_tensor_tensor(
+                    out=wbf[:, i, 0:n], in0=a3[:, i, 0:n], scalar=dis[:, i : i + 1], in1=dps[:, 0:n],
+                    op0=ALU.mult, op1=ALU.mult,
+                )
+                x, p0 = place[i]
+                for u in range(i + 1):
+                    nc.tensor.transpose(out=x[:, p0 + u, :], in_=wbf[:, i, u * P : (u + 1) * P], identity=identb[:])
+                nc.scalar.copy(
+                    out=gw4[:, i, :, 0 : i + 1],
+                    in_=x[:, p0 : p0 + i + 1, :].rearrange("p u t -> p t u"),
+                )
+            for i in (3, 2, 1, 0):
+                n = (i + 1) * P
+                hit = work.tile([P, T], BF16, name="hit")
+                nc.vector.scalar_tensor_tensor(
+                    out=hit[:, 0:n], in0=ab3[:, i, 0:n], scalar=dis[:, i : i + 1], in1=tps[:, 0:n],
+                    op0=ALU.mult, op1=ALU.is_gt, accum_out=cnt[:, i : i + 1],
+                )
+            fac = small.tile([P, NT], F32, name="fac")
+            nc.vector.tensor_scalar(
+                out=fac[:], in0=cnt[:], scalar1=0.5, scalar2=math.sqrt(GAMMA), op0=ALU.is_gt, op1=ALU.mult
+            )
+            st[("f", b)] = fac
+
+        def s2b(b):
+            gw = gws[b % NGW]
+            fac = st[("f", b)]
+            kc, ks = st[("k", b)]
+            wc = work.tile([P, NT * P], U32, name="wc", align_bytes=64)
+            ws = work.tile([P, NT * P], U8, name="ws", align_bytes=64)
+            nc.vector.quantize_mx(out=wc[:].bitcast(FP8X4), scales=ws[:], in_=gw[:])
+            o_sb = work.tile([P, NT, D], F32, name="o_sb")
+            for h in range(2):
+                ops = ps_o.tile([P, 2, D], F32, name="ops")
+                for j in range(2):
+                    i = 2 * h + j
+                    nc.tensor.matmul_mx(
+                        out=ops[:, j, :],
+                        lhsT=wc[:, i * P : (i + 1) * P].bitcast(FP8X4),
+                        lhsT_scale=ws[:, i * P : (i + 1) * P],
+                        rhs=kc[:].bitcast(FP8X4),
+                        rhs_scale=ks[:],
+                        start=True,
+                        stop=True,
+                    )
+                for j in range(2):
+                    i = 2 * h + j
+                    nc.scalar.activation(out=o_sb[:, i, :], in_=ops[:, j, :], func=ACT.Copy, scale=fac[:, i : i + 1])
+            nc.sync.dma_start(out=out[b].rearrange("(i p) d -> p i d", p=P), in_=o_sb[:])
+
+        for step in range(B + 2):
+            if step < B:
+                s1(step)
+                kprep(step)
+            if 0 <= step - 1 < B:
+                s2a(step - 1)
+            if 0 <= step - 2 < B:
+                s2b(step - 2)

@@ -41,10 +41,14 @@ def tile_symbolicpenaltytracker_kernel(tc, A_rel, k_seq, out):
         for b in range(B):
             at = resid.tile([P, NT * 640], BF16, name="a%d" % b)
             kt = resid.tile([P, NT, D], BF16, name="k%d" % b)
-            nc.sync.dma_start(
-                out=at[:, 0 : NT * T].rearrange("p (i s) -> p i s", s=T),
-                in_=A_rel[b].rearrange("(i p) s -> p i s", p=P),
-            )
+            if b == 0:
+                for i in range(NT):
+                    nc.sync.dma_start(out=at[:, i * T : (i + 1) * T], in_=A_rel[b, i * P : (i + 1) * P, :])
+            else:
+                nc.sync.dma_start(
+                    out=at[:, 0 : NT * T].rearrange("p (i s) -> p i s", s=T),
+                    in_=A_rel[b].rearrange("(i p) s -> p i s", p=P),
+                )
             nc.sync.dma_start(out=kt[:], in_=k_seq[b].rearrange("(u p) d -> p u d", p=P))
             a_sb.append(at)
             k_sb.append(kt)
@@ -76,9 +80,10 @@ def tile_symbolicpenaltytracker_kernel(tc, A_rel, k_seq, out):
 
         def kprep(b):
             kg = work.tile([P, D * 4], BF16, name="kg", align_bytes=64)
-            nc.vector.tensor_copy(
-                out=kg[:].rearrange("p (c i t) -> p c t i", i=4, t=4),
-                in_=k_sb[b][:].rearrange("p t (c i) -> p c t i", i=4),
+            nc.gpsimd.tensor_scalar(
+                out=kg[:].rearrange("p (d t) -> p d t", t=4),
+                in0=k_sb[b][:].rearrange("p t d -> p d t"),
+                scalar1=1.0, scalar2=0.0, op0=ALU.mult, op1=ALU.add,
             )
             kc = resid.tile([P, D], U32, name="kc%d" % b, align_bytes=64)
             ks = resid.tile([P, D], U8, name="ks%d" % b, align_bytes=64)
@@ -88,9 +93,18 @@ def tile_symbolicpenaltytracker_kernel(tc, A_rel, k_seq, out):
         def s1(b):
             a3 = a_sb[b][:, 0 : NT * T].rearrange("p (i s) -> p i s", s=T)
             deg = small.tile([P, NT], F32, name="deg")
-            for i in range(NT):
-                junk = work.tile([P, T], BF16, name="junk")
-                nc.scalar.activation(out=junk[:], in_=a3[:, i, :], func=ACT.Copy, accum_out=deg[:, i : i + 1])
+            if b == 0:
+                for i in range(NT):
+                    junk = work.tile([P, T], BF16, name="junk")
+                    nc.scalar.activation(out=junk[:], in_=a3[:, i, :], func=ACT.Copy, accum_out=deg[:, i : i + 1])
+            else:
+                pair = work.tile([P, NT, T // 2], F32, name="pair")
+                nc.gpsimd.tensor_tensor(out=pair[:], in0=a3[:, :, 0 : T // 2], in1=a3[:, :, T // 2 : T], op=ALU.add)
+                for i in range(NT):
+                    junk = work.tile([P, T], BF16, name="junk")
+                    nc.scalar.activation(
+                        out=junk[:, 0 : T // 2], in_=pair[:, i, :], func=ACT.Copy, accum_out=deg[:, i : i + 1]
+                    )
             sd = small.tile([P, NT], F32, name="sd")
             nc.scalar.activation(out=sd[:], in_=deg[:], func=ACT.Sqrt, bias=EPS)
             thr = small.tile([P, NT], F32, name="thr")
@@ -157,11 +171,20 @@ def tile_symbolicpenaltytracker_kernel(tc, A_rel, k_seq, out):
             gw = gws[b % NGW]
             fac = st[("f", b)]
             kc, ks = st[("k", b)]
+            last = b == B - 1
             wc = work.tile([P, NT * P], U32, name="wc", align_bytes=64)
             ws = work.tile([P, NT * P], U8, name="ws", align_bytes=64)
-            nc.vector.quantize_mx(out=wc[:].bitcast(FP8X4), scales=ws[:], in_=gw[:])
             o_sb = work.tile([P, NT, D], F32, name="o_sb")
-            for h in range(2):
+            o_dr = out[b].rearrange("(i p) d -> p i d", p=P)
+            if not last:
+                nc.vector.quantize_mx(out=wc[:].bitcast(FP8X4), scales=ws[:], in_=gw[:])
+            for h in (1, 0):
+                if last:
+                    nc.vector.quantize_mx(
+                        out=wc[:, h * 2 * P : (h + 1) * 2 * P].bitcast(FP8X4),
+                        scales=ws[:, h * 2 * P : (h + 1) * 2 * P],
+                        in_=gw[:, h * 8 * P : (h + 1) * 8 * P],
+                    )
                 ops = ps_o.tile([P, 2, D], F32, name="ops")
                 for j in range(2):
                     i = 2 * h + j
@@ -176,8 +199,16 @@ def tile_symbolicpenaltytracker_kernel(tc, A_rel, k_seq, out):
                     )
                 for j in range(2):
                     i = 2 * h + j
-                    nc.scalar.activation(out=o_sb[:, i, :], in_=ops[:, j, :], func=ACT.Copy, scale=fac[:, i : i + 1])
-            nc.sync.dma_start(out=out[b].rearrange("(i p) d -> p i d", p=P), in_=o_sb[:])
+                    if last and j == 1:
+                        nc.vector.tensor_scalar_mul(out=o_sb[:, i, :], in0=ops[:, j, :], scalar1=fac[:, i : i + 1])
+                    else:
+                        nc.scalar.activation(
+                            out=o_sb[:, i, :], in_=ops[:, j, :], func=ACT.Copy, scale=fac[:, i : i + 1]
+                        )
+                if last:
+                    nc.sync.dma_start(out=o_dr[:, 2 * h : 2 * h + 2, :], in_=o_sb[:, 2 * h : 2 * h + 2, :])
+            if not last:
+                nc.sync.dma_start(out=o_dr, in_=o_sb[:])
 
         for step in range(B + 2):
             if step < B:

@@ -12,7 +12,6 @@ I32 = mybir.dt.int32
 FP8X4 = mybir.dt.float8_e4m3fn_x4
 ALU = mybir.AluOpType
 ACT = mybir.ActivationFunctionType
-AX = mybir.AxisListType
 
 B, T, D = 8, 512, 256
 P = 128
@@ -22,6 +21,8 @@ EPS = 1e-06
 REL_THRESH = 1e-09
 FLOPS = 2 * B * T * T * D
 NGW = 3
+PAIR = []
+K_EARLY = 2
 
 
 def tile_symbolicpenaltytracker_kernel(tc, A_rel, k_seq, out):
@@ -36,22 +37,29 @@ def tile_symbolicpenaltytracker_kernel(tc, A_rel, k_seq, out):
         ps_x = ctx.enter_context(tc.psum_pool(name="ps_x", bufs=1))
         ps_o = ctx.enter_context(tc.psum_pool(name="ps_o", bufs=2))
 
-        a_sb = []
-        k_sb = []
-        for b in range(B):
-            at = resid.tile([P, NT * 640], BF16, name="a%d" % b)
-            kt = resid.tile([P, NT, D], BF16, name="k%d" % b)
+        a_sb = [resid.tile([P, NT * 640], BF16, name="a%d" % b) for b in range(B)]
+        k_sb = [resid.tile([P, NT, D], BF16, name="k%d" % b) for b in range(B)]
+
+        def load_a(b):
             if b == 0:
                 for i in range(NT):
-                    nc.sync.dma_start(out=at[:, i * T : (i + 1) * T], in_=A_rel[b, i * P : (i + 1) * P, :])
+                    nc.sync.dma_start(out=a_sb[b][:, i * T : (i + 1) * T], in_=A_rel[b, i * P : (i + 1) * P, :])
             else:
                 nc.sync.dma_start(
-                    out=at[:, 0 : NT * T].rearrange("p (i s) -> p i s", s=T),
+                    out=a_sb[b][:, 0 : NT * T].rearrange("p (i s) -> p i s", s=T),
                     in_=A_rel[b].rearrange("(i p) s -> p i s", p=P),
                 )
-            nc.sync.dma_start(out=kt[:], in_=k_seq[b].rearrange("(u p) d -> p u d", p=P))
-            a_sb.append(at)
-            k_sb.append(kt)
+
+        def load_k(b):
+            nc.sync.dma_start(out=k_sb[b][:], in_=k_seq[b].rearrange("(u p) d -> p u d", p=P))
+
+        load_a(0)
+        for b in range(K_EARLY):
+            load_k(b)
+        for b in range(1, B):
+            load_a(b)
+            if b >= K_EARLY:
+                load_k(b)
 
         warm = const.tile([P, 1], F32, name="warm")
         nc.vector.memset(warm[:], 1.0)
@@ -80,11 +88,21 @@ def tile_symbolicpenaltytracker_kernel(tc, A_rel, k_seq, out):
 
         def kprep(b):
             kg = work.tile([P, D * 4], BF16, name="kg", align_bytes=64)
-            nc.gpsimd.tensor_scalar(
-                out=kg[:].rearrange("p (d t) -> p d t", t=4),
-                in0=k_sb[b][:].rearrange("p t d -> p d t"),
-                scalar1=1.0, scalar2=0.0, op0=ALU.mult, op1=ALU.add,
-            )
+            if b < 2:
+                nc.vector.tensor_copy(
+                    out=kg[:].rearrange("p (c i t) -> p c t i", i=4, t=4),
+                    in_=k_sb[b][:].rearrange("p t (c i) -> p c t i", i=4),
+                )
+            else:
+                nc.gpsimd.tensor_scalar(
+                    out=kg[:].rearrange("p (d t) -> p d t", t=4),
+                    in0=k_sb[b][:].rearrange("p t d -> p d t"),
+                    scalar1=1.0, scalar2=0.0, op0=ALU.mult, op1=ALU.add,
+                )
+            st[("kg", b)] = kg
+
+        def kquant(b):
+            kg = st[("kg", b)]
             kc = resid.tile([P, D], U32, name="kc%d" % b, align_bytes=64)
             ks = resid.tile([P, D], U8, name="ks%d" % b, align_bytes=64)
             nc.vector.quantize_mx(out=kc[:].bitcast(FP8X4), scales=ks[:], in_=kg[:])
@@ -93,11 +111,7 @@ def tile_symbolicpenaltytracker_kernel(tc, A_rel, k_seq, out):
         def s1(b):
             a3 = a_sb[b][:, 0 : NT * T].rearrange("p (i s) -> p i s", s=T)
             deg = small.tile([P, NT], F32, name="deg")
-            if b == 0:
-                for i in range(NT):
-                    junk = work.tile([P, T], BF16, name="junk")
-                    nc.scalar.activation(out=junk[:], in_=a3[:, i, :], func=ACT.Copy, accum_out=deg[:, i : i + 1])
-            else:
+            if b in PAIR:
                 pair = work.tile([P, NT, T // 2], F32, name="pair")
                 nc.gpsimd.tensor_tensor(out=pair[:], in0=a3[:, :, 0 : T // 2], in1=a3[:, :, T // 2 : T], op=ALU.add)
                 for i in range(NT):
@@ -105,6 +119,10 @@ def tile_symbolicpenaltytracker_kernel(tc, A_rel, k_seq, out):
                     nc.scalar.activation(
                         out=junk[:, 0 : T // 2], in_=pair[:, i, :], func=ACT.Copy, accum_out=deg[:, i : i + 1]
                     )
+            else:
+                for i in range(NT):
+                    junk = work.tile([P, T], BF16, name="junk")
+                    nc.scalar.activation(out=junk[:], in_=a3[:, i, :], func=ACT.Copy, accum_out=deg[:, i : i + 1])
             sd = small.tile([P, NT], F32, name="sd")
             nc.scalar.activation(out=sd[:], in_=deg[:], func=ACT.Sqrt, bias=EPS)
             thr = small.tile([P, NT], F32, name="thr")
@@ -210,10 +228,15 @@ def tile_symbolicpenaltytracker_kernel(tc, A_rel, k_seq, out):
             if not last:
                 nc.sync.dma_start(out=o_dr, in_=o_sb[:])
 
+        for b in range(K_EARLY):
+            kprep(b)
+            kquant(b)
         for step in range(B + 2):
             if step < B:
                 s1(step)
-                kprep(step)
+                if step >= K_EARLY:
+                    kprep(step)
+                    kquant(step)
             if 0 <= step - 1 < B:
                 s2a(step - 1)
             if 0 <= step - 2 < B:

@@ -65,24 +65,24 @@ def tile_symbolicpenaltytracker_kernel(tc, A_rel, k_seq, out):
         nc.vector.memset(warm[:], 1.0)
         nc.scalar.activation(out=warm[:], in_=warm[:], func=ACT.Sqrt)
 
-        ident = const.tile([P, P], F32, name="ident")
-        make_identity(nc, ident[:])
-        identb = const.tile([P, P], BF16, name="identb")
-        make_identity(nc, identb[:])
+        gws = []
+        for j in range(NGW):
+            g = const.tile([P, NT * P * 4], BF16, name="gw%d" % j, align_bytes=64)
+            nc.vector.memset(g[:].bitcast(I32), 0)
+            gws.append(g)
+
         trilf = const.tile([P, P], F32, name="trilf")
         nc.gpsimd.memset(trilf[:], 1.0)
         nc.gpsimd.affine_select(
             out=trilf[:], in_=trilf[:], compare_op=ALU.is_ge, fill=0.0, base=0,
             pattern=[[-1, P]], channel_multiplier=1,
         )
+        ident = const.tile([P, P], F32, name="ident")
+        make_identity(nc, ident[:])
         trilb = const.tile([P, P], BF16, name="trilb")
         nc.vector.tensor_copy(out=trilb[:], in_=trilf[:])
-
-        gws = []
-        for j in range(NGW):
-            g = const.tile([P, NT * P * 4], BF16, name="gw%d" % j, align_bytes=64)
-            nc.vector.memset(g[:], 0.0)
-            gws.append(g)
+        identb = const.tile([P, P], BF16, name="identb")
+        make_identity(nc, identb[:])
 
         st = {}
 
@@ -130,7 +130,7 @@ def tile_symbolicpenaltytracker_kernel(tc, A_rel, k_seq, out):
             dis = small.tile([P, NT], F32, name="dis")
             nc.vector.reciprocal(out=dis[:], in_=sd[:])
             adiag = a_sb[b][:].rearrange("p (i x) -> p i x", x=640)[:, :, 0:P]
-            nc.gpsimd.tensor_tensor(
+            nc.vector.tensor_tensor(
                 out=adiag, in0=adiag, in1=trilb[:].unsqueeze(1).to_broadcast([P, NT, P]), op=ALU.mult
             )
             aabs = work.tile([P, NT * T], BF16, name="aabs")
@@ -185,6 +185,67 @@ def tile_symbolicpenaltytracker_kernel(tc, A_rel, k_seq, out):
             )
             st[("f", b)] = fac
 
+        def head0():
+            b = 0
+            a3 = a_sb[b][:, 0 : NT * T].rearrange("p (i s) -> p i s", s=T)
+            ai = a_sb[b][:, 0 : NT * T].bitcast(I32)
+            deg = small.tile([P, NT], F32, name="deg")
+            sd = small.tile([P, NT], F32, name="sd")
+            thr = small.tile([P, NT], F32, name="thr")
+            dis = small.tile([P, NT], F32, name="dis")
+            cnt = small.tile([P, NT], F32, name="cnt")
+            aabs = work.tile([P, NT * T], BF16, name="aabs")
+            ab3 = aabs[:].rearrange("p (i s) -> p i s", s=T)
+            abi = aabs[:].bitcast(I32)
+            dps = ps_d.tile([P, T], F32, name="dps")
+            tps = ps_t.tile([P, T], F32, name="tps")
+            wbf = work.tile([P, NT, T], BF16, name="wbf")
+            gw = gws[b % NGW]
+            gw4 = gw[:].rearrange("p (i t u) -> p i t u", t=P, u=4)
+            xa = ps_x.tile([P, 8, P], BF16, name="xa", bufs=2)
+            xb = ps_x.tile([P, 2, P], BF16, name="xb", bufs=1)
+            place = {3: (xa, 0), 2: (xa, 4), 0: (xa, 7), 1: (xb, 0)}
+            for i in range(NT):
+                n = (i + 1) * P
+                c1 = slice(i, i + 1)
+                junk = work.tile([P, T], BF16, name="junk")
+                nc.scalar.activation(out=junk[:], in_=a3[:, i, :], func=ACT.Copy, accum_out=deg[:, c1])
+                nc.scalar.activation(out=sd[:, c1], in_=deg[:, c1], func=ACT.Sqrt, bias=EPS)
+                nc.scalar.mul(out=thr[:, c1], in_=sd[:, c1], mul=REL_THRESH)
+                nc.vector.reciprocal(out=dis[:, c1], in_=sd[:, c1])
+                nc.vector.tensor_tensor(
+                    out=a3[:, i, i * P : n], in0=a3[:, i, i * P : n], in1=trilb[:], op=ALU.mult
+                )
+                w0 = i * (T // 2)
+                nc.vector.tensor_single_scalar(
+                    out=abi[:, w0 : w0 + n // 2], in_=ai[:, w0 : w0 + n // 2], scalar=0x7FFF7FFF, op=ALU.bitwise_and
+                )
+                for dst, src in ((dps, dis), (tps, thr)):
+                    nc.tensor.transpose(
+                        out=dst[:, i * P : n], in_=src[:, c1].to_broadcast([P, P]), identity=ident[:]
+                    )
+                nc.vector.scalar_tensor_tensor(
+                    out=wbf[:, i, 0:n], in0=a3[:, i, 0:n], scalar=dis[:, c1], in1=dps[:, 0:n],
+                    op0=ALU.mult, op1=ALU.mult,
+                )
+                x, p0 = place[i]
+                for u in range(i + 1):
+                    nc.tensor.transpose(out=x[:, p0 + u, :], in_=wbf[:, i, u * P : (u + 1) * P], identity=identb[:])
+                nc.scalar.copy(
+                    out=gw4[:, i, :, 0 : i + 1],
+                    in_=x[:, p0 : p0 + i + 1, :].rearrange("p u t -> p t u"),
+                )
+                hit = work.tile([P, T], BF16, name="hit")
+                nc.vector.scalar_tensor_tensor(
+                    out=hit[:, 0:n], in0=ab3[:, i, 0:n], scalar=dis[:, c1], in1=tps[:, 0:n],
+                    op0=ALU.mult, op1=ALU.is_gt, accum_out=cnt[:, c1],
+                )
+            fac = small.tile([P, NT], F32, name="fac")
+            nc.vector.tensor_scalar(
+                out=fac[:], in0=cnt[:], scalar1=0.5, scalar2=math.sqrt(GAMMA), op0=ALU.is_gt, op1=ALU.mult
+            )
+            st[("f", b)] = fac
+
         def s2b(b):
             gw = gws[b % NGW]
             fac = st[("f", b)]
@@ -228,16 +289,17 @@ def tile_symbolicpenaltytracker_kernel(tc, A_rel, k_seq, out):
             if not last:
                 nc.sync.dma_start(out=o_dr, in_=o_sb[:])
 
+        head0()
         for b in range(K_EARLY):
             kprep(b)
             kquant(b)
-        for step in range(B + 2):
+        for step in range(1, B + 2):
             if step < B:
                 s1(step)
                 if step >= K_EARLY:
                     kprep(step)
                     kquant(step)
-            if 0 <= step - 1 < B:
+            if 1 <= step - 1 < B:
                 s2a(step - 1)
             if 0 <= step - 2 < B:
                 s2b(step - 2)

@@ -6,23 +6,25 @@ from concourse.masks import make_identity
 
 F32 = mybir.dt.float32
 BF16 = mybir.dt.bfloat16
+I32 = mybir.dt.int32
 U32 = mybir.dt.uint32
 U8 = mybir.dt.uint8
-I32 = mybir.dt.int32
 FP8X4 = mybir.dt.float8_e4m3fn_x4
 ALU = mybir.AluOpType
 ACT = mybir.ActivationFunctionType
 
 B, T, D = 8, 512, 256
 P = 128
-NT = T // P
+NB = T // P
+PACK = 4
 GAMMA = 0.5
 EPS = 1e-06
 REL_THRESH = 1e-09
 FLOPS = 2 * B * T * T * D
-NGW = 3
-PAIR = []
-K_EARLY = 2
+
+DIAG_STEP = T + P
+N_GROUPED = 4
+K_ON_VECTOR = 2
 
 
 def tile_symbolicpenaltytracker_kernel(tc, A_rel, k_seq, out):
@@ -30,276 +32,255 @@ def tile_symbolicpenaltytracker_kernel(tc, A_rel, k_seq, out):
     with ExitStack() as ctx:
         const = ctx.enter_context(tc.tile_pool(name="const", bufs=1))
         resid = ctx.enter_context(tc.tile_pool(name="resid", bufs=1))
-        small = ctx.enter_context(tc.tile_pool(name="small", bufs=4))
-        work = ctx.enter_context(tc.tile_pool(name="work", bufs=3))
-        ps_d = ctx.enter_context(tc.psum_pool(name="ps_d", bufs=2))
-        ps_t = ctx.enter_context(tc.psum_pool(name="ps_t", bufs=1))
-        ps_x = ctx.enter_context(tc.psum_pool(name="ps_x", bufs=1))
-        ps_o = ctx.enter_context(tc.psum_pool(name="ps_o", bufs=2))
+        small = ctx.enter_context(tc.tile_pool(name="small", bufs=8))
+        work = ctx.enter_context(tc.tile_pool(name="work", bufs=4))
+        ps_dis = ctx.enter_context(tc.psum_pool(name="ps_dis", bufs=2))
+        ps_thr = ctx.enter_context(tc.psum_pool(name="ps_thr", bufs=1))
+        ps_wt = ctx.enter_context(tc.psum_pool(name="ps_wt", bufs=1))
+        ps_out = ctx.enter_context(tc.psum_pool(name="ps_out", bufs=2))
 
-        a_sb = [resid.tile([P, NT * 640], BF16, name="a%d" % b) for b in range(B)]
-        k_sb = [resid.tile([P, NT, D], BF16, name="k%d" % b) for b in range(B)]
+        a_sb = [resid.tile([P, NB * DIAG_STEP], BF16, name="a%d" % b) for b in range(B)]
+        k_sb = [resid.tile([P, PACK, D], BF16, name="k%d" % b) for b in range(B)]
+
+        def rows(b):
+            return a_sb[b][:, 0 : NB * T].rearrange("p (i s) -> p i s", s=T)
 
         def load_a(b):
             if b == 0:
-                for i in range(NT):
-                    nc.sync.dma_start(out=a_sb[b][:, i * T : (i + 1) * T], in_=A_rel[b, i * P : (i + 1) * P, :])
+                for i in range(NB):
+                    nc.sync.dma_start(out=rows(b)[:, i, :], in_=A_rel[b, i * P : (i + 1) * P, :])
             else:
-                nc.sync.dma_start(
-                    out=a_sb[b][:, 0 : NT * T].rearrange("p (i s) -> p i s", s=T),
-                    in_=A_rel[b].rearrange("(i p) s -> p i s", p=P),
-                )
+                nc.sync.dma_start(out=rows(b), in_=A_rel[b].rearrange("(i p) s -> p i s", p=P))
 
         def load_k(b):
             nc.sync.dma_start(out=k_sb[b][:], in_=k_seq[b].rearrange("(u p) d -> p u d", p=P))
 
         load_a(0)
-        for b in range(K_EARLY):
+        for b in range(K_ON_VECTOR):
             load_k(b)
         for b in range(1, B):
             load_a(b)
-            if b >= K_EARLY:
+            if b >= K_ON_VECTOR:
                 load_k(b)
 
         warm = const.tile([P, 1], F32, name="warm")
         nc.vector.memset(warm[:], 1.0)
         nc.scalar.activation(out=warm[:], in_=warm[:], func=ACT.Sqrt)
 
-        gws = []
-        for j in range(NGW):
-            g = const.tile([P, NT * P * 4], BF16, name="gw%d" % j, align_bytes=64)
+        grouped = []
+        for j in range(N_GROUPED):
+            g = const.tile([P, NB * P * PACK], BF16, name="grouped%d" % j, align_bytes=64)
             nc.vector.memset(g[:].bitcast(I32), 0)
-            gws.append(g)
+            grouped.append(g)
 
-        trilf = const.tile([P, P], F32, name="trilf")
-        nc.gpsimd.memset(trilf[:], 1.0)
+        tril_f = const.tile([P, P], F32, name="tril_f")
+        nc.gpsimd.memset(tril_f[:], 1.0)
         nc.gpsimd.affine_select(
-            out=trilf[:], in_=trilf[:], compare_op=ALU.is_ge, fill=0.0, base=0,
+            out=tril_f[:], in_=tril_f[:], compare_op=ALU.is_ge, fill=0.0, base=0,
             pattern=[[-1, P]], channel_multiplier=1,
         )
-        ident = const.tile([P, P], F32, name="ident")
-        make_identity(nc, ident[:])
-        trilb = const.tile([P, P], BF16, name="trilb")
-        nc.vector.tensor_copy(out=trilb[:], in_=trilf[:])
-        identb = const.tile([P, P], BF16, name="identb")
-        make_identity(nc, identb[:])
+        ident_f = const.tile([P, P], F32, name="ident_f")
+        make_identity(nc, ident_f[:])
+        tril = const.tile([P, P], BF16, name="tril")
+        nc.vector.tensor_copy(out=tril[:], in_=tril_f[:])
+        ident_b = const.tile([P, P], BF16, name="ident_b")
+        make_identity(nc, ident_b[:])
 
-        st = {}
+        state = {}
+        k_codes = {}
 
-        def kprep(b):
-            kg = work.tile([P, D * 4], BF16, name="kg", align_bytes=64)
-            if b < 2:
+        def prepare_k(b):
+            kg = work.tile([P, D * PACK], BF16, name="kg", align_bytes=64)
+            if b < K_ON_VECTOR:
                 nc.vector.tensor_copy(
-                    out=kg[:].rearrange("p (c i t) -> p c t i", i=4, t=4),
-                    in_=k_sb[b][:].rearrange("p t (c i) -> p c t i", i=4),
+                    out=kg[:].rearrange("p (c i u) -> p c u i", i=4, u=PACK),
+                    in_=k_sb[b][:].rearrange("p u (c i) -> p c u i", i=4),
                 )
             else:
                 nc.gpsimd.tensor_scalar(
-                    out=kg[:].rearrange("p (d t) -> p d t", t=4),
-                    in0=k_sb[b][:].rearrange("p t d -> p d t"),
+                    out=kg[:].rearrange("p (d u) -> p d u", u=PACK),
+                    in0=k_sb[b][:].rearrange("p u d -> p d u"),
                     scalar1=1.0, scalar2=0.0, op0=ALU.mult, op1=ALU.add,
                 )
-            st[("kg", b)] = kg
+            codes = resid.tile([P, D], U32, name="kc%d" % b, align_bytes=64)
+            scales = resid.tile([P, D], U8, name="ks%d" % b, align_bytes=64)
+            nc.vector.quantize_mx(out=codes[:].bitcast(FP8X4), scales=scales[:], in_=kg[:])
+            k_codes[b] = (codes, scales)
 
-        def kquant(b):
-            kg = st[("kg", b)]
-            kc = resid.tile([P, D], U32, name="kc%d" % b, align_bytes=64)
-            ks = resid.tile([P, D], U8, name="ks%d" % b, align_bytes=64)
-            nc.vector.quantize_mx(out=kc[:].bitcast(FP8X4), scales=ks[:], in_=kg[:])
-            st[("k", b)] = (kc, ks)
+        ALL = list(range(NB))
 
-        def s1(b):
-            a3 = a_sb[b][:, 0 : NT * T].rearrange("p (i s) -> p i s", s=T)
-            deg = small.tile([P, NT], F32, name="deg")
-            if b in PAIR:
-                pair = work.tile([P, NT, T // 2], F32, name="pair")
-                nc.gpsimd.tensor_tensor(out=pair[:], in0=a3[:, :, 0 : T // 2], in1=a3[:, :, T // 2 : T], op=ALU.add)
-                for i in range(NT):
-                    junk = work.tile([P, T], BF16, name="junk")
-                    nc.scalar.activation(
-                        out=junk[:, 0 : T // 2], in_=pair[:, i, :], func=ACT.Copy, accum_out=deg[:, i : i + 1]
-                    )
-            else:
-                for i in range(NT):
-                    junk = work.tile([P, T], BF16, name="junk")
-                    nc.scalar.activation(out=junk[:], in_=a3[:, i, :], func=ACT.Copy, accum_out=deg[:, i : i + 1])
-            sd = small.tile([P, NT], F32, name="sd")
-            nc.scalar.activation(out=sd[:], in_=deg[:], func=ACT.Sqrt, bias=EPS)
-            thr = small.tile([P, NT], F32, name="thr")
-            nc.scalar.mul(out=thr[:], in_=sd[:], mul=REL_THRESH)
-            dis = small.tile([P, NT], F32, name="dis")
-            nc.vector.reciprocal(out=dis[:], in_=sd[:])
-            adiag = a_sb[b][:].rearrange("p (i x) -> p i x", x=640)[:, :, 0:P]
-            nc.vector.tensor_tensor(
-                out=adiag, in0=adiag, in1=trilb[:].unsqueeze(1).to_broadcast([P, NT, P]), op=ALU.mult
-            )
-            aabs = work.tile([P, NT * T], BF16, name="aabs")
-            nc.vector.tensor_single_scalar(
-                out=aabs[:].bitcast(I32), in_=a_sb[b][:, 0 : NT * T].bitcast(I32), scalar=0x7FFF7FFF, op=ALU.bitwise_and
-            )
-            dps = ps_d.tile([P, T], F32, name="dps")
-            tps = ps_t.tile([P, T], F32, name="tps")
-            for dst, src in ((dps, dis), (tps, thr)):
-                for m in range(NT):
-                    nc.tensor.transpose(
-                        out=dst[:, m * P : (m + 1) * P],
-                        in_=src[:, m : m + 1].to_broadcast([P, P]),
-                        identity=ident[:],
-                    )
-            st[("d", b)] = (dis, dps, tps, aabs)
+        def row_sums(b, blocks):
+            if b not in state:
+                state[b] = {
+                    "deg": small.tile([P, NB], F32, name="deg"),
+                    "sd": small.tile([P, NB], F32, name="sd"),
+                }
+            s = state[b]
+            for i in blocks:
+                unused = work.tile([P, T], BF16, name="unused")
+                nc.scalar.activation(
+                    out=unused[:], in_=rows(b)[:, i, :], func=ACT.Copy, accum_out=s["deg"][:, i : i + 1]
+                )
+            c = slice(blocks[0], blocks[-1] + 1)
+            nc.scalar.activation(out=s["sd"][:, c], in_=s["deg"][:, c], func=ACT.Sqrt, bias=EPS)
 
-        def s2a(b):
-            a3 = a_sb[b][:, 0 : NT * T].rearrange("p (i s) -> p i s", s=T)
-            dis, dps, tps, aabs = st[("d", b)]
-            ab3 = aabs[:].rearrange("p (i s) -> p i s", s=T)
-            wbf = work.tile([P, NT, T], BF16, name="wbf")
-            cnt = small.tile([P, NT], F32, name="cnt")
-            gw = gws[b % NGW]
-            gw4 = gw[:].rearrange("p (i t u) -> p i t u", t=P, u=4)
-            xa = ps_x.tile([P, 8, P], BF16, name="xa", bufs=2)
-            xb = ps_x.tile([P, 2, P], BF16, name="xb", bufs=1)
-            place = {3: (xa, 0), 2: (xa, 4), 0: (xa, 7), 1: (xb, 0)}
-            for i in (3, 2, 1, 0):
+        def scales(b, blocks):
+            s = state[b]
+            if "dis" not in s:
+                s["thr"] = small.tile([P, NB], F32, name="thr")
+                s["dis"] = small.tile([P, NB], F32, name="dis")
+            c = slice(blocks[0], blocks[-1] + 1)
+            nc.vector.reciprocal(out=s["dis"][:, c], in_=s["sd"][:, c])
+            nc.vector.tensor_scalar_mul(out=s["thr"][:, c], in0=s["sd"][:, c], scalar1=REL_THRESH)
+
+        def mask_and_abs(b, blocks):
+            s = state[b]
+            if "abs" not in s:
+                s["abs"] = work.tile([P, NB * T], BF16, name="a_abs")
+            a_words = a_sb[b][:, 0 : NB * T].bitcast(I32)
+            abs_words = s["abs"][:].bitcast(I32)
+            if len(blocks) == 1:
+                i = blocks[0]
                 n = (i + 1) * P
-                nc.vector.scalar_tensor_tensor(
-                    out=wbf[:, i, 0:n], in0=a3[:, i, 0:n], scalar=dis[:, i : i + 1], in1=dps[:, 0:n],
-                    op0=ALU.mult, op1=ALU.mult,
-                )
-                x, p0 = place[i]
-                for u in range(i + 1):
-                    nc.tensor.transpose(out=x[:, p0 + u, :], in_=wbf[:, i, u * P : (u + 1) * P], identity=identb[:])
-                nc.scalar.copy(
-                    out=gw4[:, i, :, 0 : i + 1],
-                    in_=x[:, p0 : p0 + i + 1, :].rearrange("p u t -> p t u"),
-                )
-            for i in (3, 2, 1, 0):
-                n = (i + 1) * P
-                hit = work.tile([P, T], BF16, name="hit")
-                nc.vector.scalar_tensor_tensor(
-                    out=hit[:, 0:n], in0=ab3[:, i, 0:n], scalar=dis[:, i : i + 1], in1=tps[:, 0:n],
-                    op0=ALU.mult, op1=ALU.is_gt, accum_out=cnt[:, i : i + 1],
-                )
-            fac = small.tile([P, NT], F32, name="fac")
-            nc.vector.tensor_scalar(
-                out=fac[:], in0=cnt[:], scalar1=0.5, scalar2=math.sqrt(GAMMA), op0=ALU.is_gt, op1=ALU.mult
-            )
-            st[("f", b)] = fac
-
-        def head0():
-            b = 0
-            a3 = a_sb[b][:, 0 : NT * T].rearrange("p (i s) -> p i s", s=T)
-            ai = a_sb[b][:, 0 : NT * T].bitcast(I32)
-            deg = small.tile([P, NT], F32, name="deg")
-            sd = small.tile([P, NT], F32, name="sd")
-            thr = small.tile([P, NT], F32, name="thr")
-            dis = small.tile([P, NT], F32, name="dis")
-            cnt = small.tile([P, NT], F32, name="cnt")
-            aabs = work.tile([P, NT * T], BF16, name="aabs")
-            ab3 = aabs[:].rearrange("p (i s) -> p i s", s=T)
-            abi = aabs[:].bitcast(I32)
-            dps = ps_d.tile([P, T], F32, name="dps")
-            tps = ps_t.tile([P, T], F32, name="tps")
-            wbf = work.tile([P, NT, T], BF16, name="wbf")
-            gw = gws[b % NGW]
-            gw4 = gw[:].rearrange("p (i t u) -> p i t u", t=P, u=4)
-            xa = ps_x.tile([P, 8, P], BF16, name="xa", bufs=2)
-            xb = ps_x.tile([P, 2, P], BF16, name="xb", bufs=1)
-            place = {3: (xa, 0), 2: (xa, 4), 0: (xa, 7), 1: (xb, 0)}
-            for i in range(NT):
-                n = (i + 1) * P
-                c1 = slice(i, i + 1)
-                junk = work.tile([P, T], BF16, name="junk")
-                nc.scalar.activation(out=junk[:], in_=a3[:, i, :], func=ACT.Copy, accum_out=deg[:, c1])
-                nc.scalar.activation(out=sd[:, c1], in_=deg[:, c1], func=ACT.Sqrt, bias=EPS)
-                nc.scalar.mul(out=thr[:, c1], in_=sd[:, c1], mul=REL_THRESH)
-                nc.vector.reciprocal(out=dis[:, c1], in_=sd[:, c1])
-                nc.vector.tensor_tensor(
-                    out=a3[:, i, i * P : n], in0=a3[:, i, i * P : n], in1=trilb[:], op=ALU.mult
-                )
+                diag = rows(b)[:, i, i * P : n]
+                nc.vector.tensor_tensor(out=diag, in0=diag, in1=tril[:], op=ALU.mult)
                 w0 = i * (T // 2)
                 nc.vector.tensor_single_scalar(
-                    out=abi[:, w0 : w0 + n // 2], in_=ai[:, w0 : w0 + n // 2], scalar=0x7FFF7FFF, op=ALU.bitwise_and
+                    out=abs_words[:, w0 : w0 + n // 2], in_=a_words[:, w0 : w0 + n // 2],
+                    scalar=0x7FFF7FFF, op=ALU.bitwise_and,
                 )
-                for dst, src in ((dps, dis), (tps, thr)):
-                    nc.tensor.transpose(
-                        out=dst[:, i * P : n], in_=src[:, c1].to_broadcast([P, P]), identity=ident[:]
+            else:
+                diag = a_sb[b][:].rearrange("p (i x) -> p i x", x=DIAG_STEP)[:, :, 0:P]
+                nc.vector.tensor_tensor(
+                    out=diag, in0=diag, in1=tril[:].unsqueeze(1).to_broadcast([P, NB, P]), op=ALU.mult
+                )
+                a_halves = a_words.rearrange("p (h i w) -> p h i w", h=2, i=2)
+                abs_halves = abs_words.rearrange("p (h i w) -> p h i w", h=2, i=2)
+                for h in range(2):
+                    nw = (h + 1) * P
+                    nc.vector.tensor_single_scalar(
+                        out=abs_halves[:, h, :, 0:nw], in_=a_halves[:, h, :, 0:nw],
+                        scalar=0x7FFF7FFF, op=ALU.bitwise_and,
                     )
-                nc.vector.scalar_tensor_tensor(
-                    out=wbf[:, i, 0:n], in0=a3[:, i, 0:n], scalar=dis[:, c1], in1=dps[:, 0:n],
-                    op0=ALU.mult, op1=ALU.mult,
-                )
-                x, p0 = place[i]
-                for u in range(i + 1):
-                    nc.tensor.transpose(out=x[:, p0 + u, :], in_=wbf[:, i, u * P : (u + 1) * P], identity=identb[:])
-                nc.scalar.copy(
-                    out=gw4[:, i, :, 0 : i + 1],
-                    in_=x[:, p0 : p0 + i + 1, :].rearrange("p u t -> p t u"),
-                )
-                hit = work.tile([P, T], BF16, name="hit")
-                nc.vector.scalar_tensor_tensor(
-                    out=hit[:, 0:n], in0=ab3[:, i, 0:n], scalar=dis[:, c1], in1=tps[:, 0:n],
-                    op0=ALU.mult, op1=ALU.is_gt, accum_out=cnt[:, c1],
-                )
-            fac = small.tile([P, NT], F32, name="fac")
-            nc.vector.tensor_scalar(
-                out=fac[:], in0=cnt[:], scalar1=0.5, scalar2=math.sqrt(GAMMA), op0=ALU.is_gt, op1=ALU.mult
-            )
-            st[("f", b)] = fac
 
-        def s2b(b):
-            gw = gws[b % NGW]
-            fac = st[("f", b)]
-            kc, ks = st[("k", b)]
+        def spread(b, blocks):
+            s = state[b]
+            if "dis_all" not in s:
+                s["dis_all"] = ps_dis.tile([P, T], F32, name="dis_all")
+                s["thr_all"] = ps_thr.tile([P, T], F32, name="thr_all")
+            for dst, src in ((s["dis_all"], s["dis"]), (s["thr_all"], s["thr"])):
+                for i in blocks:
+                    nc.tensor.transpose(
+                        out=dst[:, i * P : (i + 1) * P],
+                        in_=src[:, i : i + 1].to_broadcast([P, P]),
+                        identity=ident_f[:],
+                    )
+
+        def weights(b, i):
+            s = state[b]
+            if "w" not in s:
+                s["w"] = work.tile([P, NB, T], BF16, name="w")
+                wt_a = ps_wt.tile([P, 8, P], BF16, name="wt_a", bufs=2)
+                wt_b = ps_wt.tile([P, 2, P], BF16, name="wt_b", bufs=1)
+                s["wt"] = {3: (wt_a, 0), 2: (wt_a, 4), 0: (wt_a, 7), 1: (wt_b, 0)}
+            n = (i + 1) * P
+            nc.vector.scalar_tensor_tensor(
+                out=s["w"][:, i, 0:n], in0=rows(b)[:, i, 0:n], scalar=s["dis"][:, i : i + 1],
+                in1=s["dis_all"][:, 0:n], op0=ALU.mult, op1=ALU.mult,
+            )
+            wt, first = s["wt"][i]
+            for u in range(i + 1):
+                nc.tensor.transpose(
+                    out=wt[:, first + u, :], in_=s["w"][:, i, u * P : (u + 1) * P], identity=ident_b[:]
+                )
+            g = grouped[b % N_GROUPED][:].rearrange("p (i t u) -> p i t u", t=P, u=PACK)
+            nc.scalar.copy(
+                out=g[:, i, :, 0 : i + 1], in_=wt[:, first : first + i + 1, :].rearrange("p u t -> p t u")
+            )
+
+        def count(b, i):
+            s = state[b]
+            if "cnt" not in s:
+                s["cnt"] = small.tile([P, NB], F32, name="cnt")
+            n = (i + 1) * P
+            hits = work.tile([P, T], BF16, name="hits")
+            nc.vector.scalar_tensor_tensor(
+                out=hits[:, 0:n], in0=s["abs"][:].rearrange("p (i s) -> p i s", s=T)[:, i, 0:n],
+                scalar=s["dis"][:, i : i + 1], in1=s["thr_all"][:, 0:n],
+                op0=ALU.mult, op1=ALU.is_gt, accum_out=s["cnt"][:, i : i + 1],
+            )
+
+        def factor(b):
+            s = state[b]
+            s["fac"] = small.tile([P, NB], F32, name="fac")
+            nc.vector.tensor_scalar(
+                out=s["fac"][:], in0=s["cnt"][:], scalar1=0.5, scalar2=math.sqrt(GAMMA),
+                op0=ALU.is_gt, op1=ALU.mult,
+            )
+
+        def product(b):
+            s = state[b]
+            g = grouped[b % N_GROUPED]
+            kc, ks = k_codes[b]
             last = b == B - 1
-            wc = work.tile([P, NT * P], U32, name="wc", align_bytes=64)
-            ws = work.tile([P, NT * P], U8, name="ws", align_bytes=64)
-            o_sb = work.tile([P, NT, D], F32, name="o_sb")
-            o_dr = out[b].rearrange("(i p) d -> p i d", p=P)
+            codes = work.tile([P, NB * P], U32, name="wc", align_bytes=64)
+            scl = work.tile([P, NB * P], U8, name="ws", align_bytes=64)
+            res = work.tile([P, NB, D], F32, name="res")
+            dst = out[b].rearrange("(i p) d -> p i d", p=P)
             if not last:
-                nc.vector.quantize_mx(out=wc[:].bitcast(FP8X4), scales=ws[:], in_=gw[:])
+                nc.vector.quantize_mx(out=codes[:].bitcast(FP8X4), scales=scl[:], in_=g[:])
             for h in (1, 0):
                 if last:
+                    c = slice(h * 2 * P, (h + 1) * 2 * P)
                     nc.vector.quantize_mx(
-                        out=wc[:, h * 2 * P : (h + 1) * 2 * P].bitcast(FP8X4),
-                        scales=ws[:, h * 2 * P : (h + 1) * 2 * P],
-                        in_=gw[:, h * 8 * P : (h + 1) * 8 * P],
+                        out=codes[:, c].bitcast(FP8X4), scales=scl[:, c],
+                        in_=g[:, h * 2 * P * PACK : (h + 1) * 2 * P * PACK],
                     )
-                ops = ps_o.tile([P, 2, D], F32, name="ops")
+                acc = ps_out.tile([P, 2, D], F32, name="acc")
                 for j in range(2):
-                    i = 2 * h + j
+                    c = slice((2 * h + j) * P, (2 * h + j + 1) * P)
                     nc.tensor.matmul_mx(
-                        out=ops[:, j, :],
-                        lhsT=wc[:, i * P : (i + 1) * P].bitcast(FP8X4),
-                        lhsT_scale=ws[:, i * P : (i + 1) * P],
-                        rhs=kc[:].bitcast(FP8X4),
-                        rhs_scale=ks[:],
-                        start=True,
-                        stop=True,
+                        out=acc[:, j, :],
+                        lhsT=codes[:, c].bitcast(FP8X4), lhsT_scale=scl[:, c],
+                        rhs=kc[:].bitcast(FP8X4), rhs_scale=ks[:],
+                        start=True, stop=True,
                     )
                 for j in range(2):
                     i = 2 * h + j
                     if last and j == 1:
-                        nc.vector.tensor_scalar_mul(out=o_sb[:, i, :], in0=ops[:, j, :], scalar1=fac[:, i : i + 1])
+                        nc.vector.tensor_scalar_mul(out=res[:, i, :], in0=acc[:, j, :], scalar1=s["fac"][:, i : i + 1])
                     else:
                         nc.scalar.activation(
-                            out=o_sb[:, i, :], in_=ops[:, j, :], func=ACT.Copy, scale=fac[:, i : i + 1]
+                            out=res[:, i, :], in_=acc[:, j, :], func=ACT.Copy, scale=s["fac"][:, i : i + 1]
                         )
                 if last:
-                    nc.sync.dma_start(out=o_dr[:, 2 * h : 2 * h + 2, :], in_=o_sb[:, 2 * h : 2 * h + 2, :])
+                    nc.sync.dma_start(out=dst[:, 2 * h : 2 * h + 2, :], in_=res[:, 2 * h : 2 * h + 2, :])
             if not last:
-                nc.sync.dma_start(out=o_dr, in_=o_sb[:])
+                nc.sync.dma_start(out=dst, in_=res[:])
 
-        head0()
-        for b in range(K_EARLY):
-            kprep(b)
-            kquant(b)
-        for step in range(1, B + 2):
-            if step < B:
-                s1(step)
-                if step >= K_EARLY:
-                    kprep(step)
-                    kquant(step)
-            if 1 <= step - 1 < B:
-                s2a(step - 1)
-            if 0 <= step - 2 < B:
-                s2b(step - 2)
+        for i in ALL:
+            row_sums(0, [i])
+            scales(0, [i])
+            mask_and_abs(0, [i])
+            spread(0, [i])
+            weights(0, i)
+            count(0, i)
+        factor(0)
+        for b in range(K_ON_VECTOR):
+            prepare_k(b)
+        for b in range(1, B + 2):
+            if b < B:
+                row_sums(b, ALL)
+                scales(b, ALL)
+                mask_and_abs(b, ALL)
+                spread(b, ALL)
+                if b >= K_ON_VECTOR:
+                    prepare_k(b)
+            if 1 <= b - 1 < B:
+                for i in reversed(ALL):
+                    weights(b - 1, i)
+                for i in reversed(ALL):
+                    count(b - 1, i)
+                factor(b - 1)
+            if b - 2 >= 0:
+                product(b - 2)

@@ -23,7 +23,7 @@ REL_THRESH = 1e-09
 FLOPS = 2 * B * T * T * D
 
 DIAG_STEP = T + P
-N_GROUPED = 4
+N_GROUPED = 3
 K_ON_VECTOR = 2
 
 
@@ -32,8 +32,8 @@ def tile_symbolicpenaltytracker_kernel(tc, A_rel, k_seq, out):
     with ExitStack() as ctx:
         const = ctx.enter_context(tc.tile_pool(name="const", bufs=1))
         resid = ctx.enter_context(tc.tile_pool(name="resid", bufs=1))
-        small = ctx.enter_context(tc.tile_pool(name="small", bufs=8))
-        work = ctx.enter_context(tc.tile_pool(name="work", bufs=4))
+        small = ctx.enter_context(tc.tile_pool(name="small", bufs=4))
+        work = ctx.enter_context(tc.tile_pool(name="work", bufs=3))
         ps_dis = ctx.enter_context(tc.psum_pool(name="ps_dis", bufs=2))
         ps_thr = ctx.enter_context(tc.psum_pool(name="ps_thr", bufs=1))
         ps_wt = ctx.enter_context(tc.psum_pool(name="ps_wt", bufs=1))
@@ -114,6 +114,7 @@ def tile_symbolicpenaltytracker_kernel(tc, A_rel, k_seq, out):
                 state[b] = {
                     "deg": small.tile([P, NB], F32, name="deg"),
                     "sd": small.tile([P, NB], F32, name="sd"),
+                    "thr": small.tile([P, NB], F32, name="thr"),
                 }
             s = state[b]
             for i in blocks:
@@ -123,15 +124,14 @@ def tile_symbolicpenaltytracker_kernel(tc, A_rel, k_seq, out):
                 )
             c = slice(blocks[0], blocks[-1] + 1)
             nc.scalar.activation(out=s["sd"][:, c], in_=s["deg"][:, c], func=ACT.Sqrt, bias=EPS)
+            nc.scalar.mul(out=s["thr"][:, c], in_=s["sd"][:, c], mul=REL_THRESH)
 
         def scales(b, blocks):
             s = state[b]
             if "dis" not in s:
-                s["thr"] = small.tile([P, NB], F32, name="thr")
                 s["dis"] = small.tile([P, NB], F32, name="dis")
             c = slice(blocks[0], blocks[-1] + 1)
             nc.vector.reciprocal(out=s["dis"][:, c], in_=s["sd"][:, c])
-            nc.vector.tensor_scalar_mul(out=s["thr"][:, c], in0=s["sd"][:, c], scalar1=REL_THRESH)
 
         def mask_and_abs(b, blocks):
             s = state[b]
@@ -154,14 +154,7 @@ def tile_symbolicpenaltytracker_kernel(tc, A_rel, k_seq, out):
                 nc.vector.tensor_tensor(
                     out=diag, in0=diag, in1=tril[:].unsqueeze(1).to_broadcast([P, NB, P]), op=ALU.mult
                 )
-                a_halves = a_words.rearrange("p (h i w) -> p h i w", h=2, i=2)
-                abs_halves = abs_words.rearrange("p (h i w) -> p h i w", h=2, i=2)
-                for h in range(2):
-                    nw = (h + 1) * P
-                    nc.vector.tensor_single_scalar(
-                        out=abs_halves[:, h, :, 0:nw], in_=a_halves[:, h, :, 0:nw],
-                        scalar=0x7FFF7FFF, op=ALU.bitwise_and,
-                    )
+                nc.vector.tensor_single_scalar(out=abs_words, in_=a_words, scalar=0x7FFF7FFF, op=ALU.bitwise_and)
 
         def spread(b, blocks):
             s = state[b]
@@ -213,7 +206,8 @@ def tile_symbolicpenaltytracker_kernel(tc, A_rel, k_seq, out):
         def factor(b):
             s = state[b]
             s["fac"] = small.tile([P, NB], F32, name="fac")
-            nc.vector.tensor_scalar(
+            engine = nc.vector if b == B - 1 else nc.gpsimd
+            engine.tensor_scalar(
                 out=s["fac"][:], in0=s["cnt"][:], scalar1=0.5, scalar2=math.sqrt(GAMMA),
                 op0=ALU.is_gt, op1=ALU.mult,
             )

@@ -102,10 +102,14 @@ def tile_symbolicpenaltytracker_kernel(tc, A_rel, k_seq, out):
                     in0=k_sb[b][:].rearrange("p u d -> p d u"),
                     scalar1=1.0, scalar2=0.0, op0=ALU.mult, op1=ALU.add,
                 )
-            codes = resid.tile([P, D], U32, name="kc%d" % b, align_bytes=64)
-            scales = resid.tile([P, D], U8, name="ks%d" % b, align_bytes=64)
-            nc.vector.quantize_mx(out=codes[:].bitcast(FP8X4), scales=scales[:], in_=kg[:])
-            k_codes[b] = (codes, scales)
+            if b % 2 == 0:
+                k_codes[b // 2] = (
+                    resid.tile([P, 2 * D], U32, name="kc%d" % b, align_bytes=64),
+                    resid.tile([P, 2 * D], U8, name="ks%d" % b, align_bytes=64),
+                )
+            codes, scales = k_codes[b // 2]
+            c = slice((b % 2) * D, (b % 2 + 1) * D)
+            nc.vector.quantize_mx(out=codes[:, c].bitcast(FP8X4), scales=scales[:, c], in_=kg[:])
 
         ALL = list(range(NB))
 
@@ -215,7 +219,8 @@ def tile_symbolicpenaltytracker_kernel(tc, A_rel, k_seq, out):
         def product(b):
             s = state[b]
             g = grouped[b % N_GROUPED]
-            kc, ks = k_codes[b]
+            kc, ks = k_codes[b // 2]
+            mine = slice((b % 2) * D, (b % 2 + 1) * D)
             last = b == B - 1
             codes = work.tile([P, NB * P], U32, name="wc", align_bytes=64)
             scl = work.tile([P, NB * P], U8, name="ws", align_bytes=64)
@@ -230,11 +235,13 @@ def tile_symbolicpenaltytracker_kernel(tc, A_rel, k_seq, out):
                         out=codes[:, c].bitcast(FP8X4), scales=scl[:, c],
                         in_=g[:, h * 2 * P * PACK : (h + 1) * 2 * P * PACK],
                     )
-                acc = ps_out.tile([P, 2, D], F32, name="acc")
+                accs = []
                 for j in range(2):
                     c = slice((2 * h + j) * P, (2 * h + j + 1) * P)
+                    acc = ps_out.tile([P, 2 * D], F32, name="acc")
+                    accs.append(acc)
                     nc.tensor.matmul_mx(
-                        out=acc[:, j, :],
+                        out=acc[:],
                         lhsT=codes[:, c].bitcast(FP8X4), lhsT_scale=scl[:, c],
                         rhs=kc[:].bitcast(FP8X4), rhs_scale=ks[:],
                         start=True, stop=True,
@@ -242,10 +249,10 @@ def tile_symbolicpenaltytracker_kernel(tc, A_rel, k_seq, out):
                 for j in range(2):
                     i = 2 * h + j
                     if last and j == 1:
-                        nc.vector.tensor_scalar_mul(out=res[:, i, :], in0=acc[:, j, :], scalar1=s["fac"][:, i : i + 1])
+                        nc.vector.tensor_scalar_mul(out=res[:, i, :], in0=accs[j][:, mine], scalar1=s["fac"][:, i : i + 1])
                     else:
                         nc.scalar.activation(
-                            out=res[:, i, :], in_=acc[:, j, :], func=ACT.Copy, scale=s["fac"][:, i : i + 1]
+                            out=res[:, i, :], in_=accs[j][:, mine], func=ACT.Copy, scale=s["fac"][:, i : i + 1]
                         )
                 if last:
                     nc.sync.dma_start(out=dst[:, 2 * h : 2 * h + 2, :], in_=res[:, 2 * h : 2 * h + 2, :])

import math
from contextlib import ExitStack

import concourse.mybir as mybir
from concourse.masks import make_identity

F32 = mybir.dt.float32
BF16 = mybir.dt.bfloat16
I32 = mybir.dt.int32
U32 = mybir.dt.uint32
U8 = mybir.dt.uint8
FP8X4 = mybir.dt.float8_e4m3fn_x4
ALU = mybir.AluOpType
ACT = mybir.ActivationFunctionType

B, T, D = 8, 512, 256
P = 128
NB = T // P
PACK = 4
GAMMA = 0.5
EPS = 1e-06
REL_THRESH = 1e-09
FLOPS = 2 * B * T * T * D

DIAG_STEP = T + P
N_GROUPED = 3
K_ON_VECTOR = 2


def tile_symbolicpenaltytracker_kernel(tc, A_rel, k_seq, out):
    nc = tc.nc
    with ExitStack() as ctx:
        const = ctx.enter_context(tc.tile_pool(name="const", bufs=1))
        resid = ctx.enter_context(tc.tile_pool(name="resid", bufs=1))
        small = ctx.enter_context(tc.tile_pool(name="small", bufs=4))
        work = ctx.enter_context(tc.tile_pool(name="work", bufs=3))
        ps_dis = ctx.enter_context(tc.psum_pool(name="ps_dis", bufs=2))
        ps_thr = ctx.enter_context(tc.psum_pool(name="ps_thr", bufs=1))
        ps_wt = ctx.enter_context(tc.psum_pool(name="ps_wt", bufs=1))
        ps_out = ctx.enter_context(tc.psum_pool(name="ps_out", bufs=2))

        a_sb = [resid.tile([P, NB * DIAG_STEP], BF16, name="a%d" % b) for b in range(B)]
        k_sb = [resid.tile([P, PACK, D], BF16, name="k%d" % b) for b in range(B)]

        def rows(b):
            return a_sb[b][:, 0 : NB * T].rearrange("p (i s) -> p i s", s=T)

        def load_a(b):
            if b == 0:
                for i in range(NB):
                    nc.sync.dma_start(out=rows(b)[:, i, :], in_=A_rel[b, i * P : (i + 1) * P, :])
            else:
                nc.sync.dma_start(out=rows(b), in_=A_rel[b].rearrange("(i p) s -> p i s", p=P))

        def load_k(b):
            nc.sync.dma_start(out=k_sb[b][:], in_=k_seq[b].rearrange("(u p) d -> p u d", p=P))

        load_a(0)
        for b in range(K_ON_VECTOR):
            load_k(b)
        for b in range(1, B):
            load_a(b)
            if b >= K_ON_VECTOR:
                load_k(b)

        warm = const.tile([P, 1], F32, name="warm")
        nc.vector.memset(warm[:], 1.0)
        nc.scalar.activation(out=warm[:], in_=warm[:], func=ACT.Sqrt)

        grouped = []
        for j in range(N_GROUPED):
            g = const.tile([P, NB * P * PACK], BF16, name="grouped%d" % j, align_bytes=64)
            nc.vector.memset(g[:].bitcast(I32), 0)
            grouped.append(g)

        tril_f = const.tile([P, P], F32, name="tril_f")
        nc.gpsimd.memset(tril_f[:], 1.0)
        nc.gpsimd.affine_select(
            out=tril_f[:], in_=tril_f[:], compare_op=ALU.is_ge, fill=0.0, base=0,
            pattern=[[-1, P]], channel_multiplier=1,
        )
        ident_f = const.tile([P, P], F32, name="ident_f")
        make_identity(nc, ident_f[:])
        tril = const.tile([P, P], BF16, name="tril")
        nc.vector.tensor_copy(out=tril[:], in_=tril_f[:])
        ident_b = const.tile([P, P], BF16, name="ident_b")
        make_identity(nc, ident_b[:])

        state = {}
        k_codes = {}

        def prepare_k(b):
            kg = work.tile([P, D * PACK], BF16, name="kg", align_bytes=64)
            if b < K_ON_VECTOR:
                nc.vector.tensor_copy(
                    out=kg[:].rearrange("p (c i u) -> p c u i", i=4, u=PACK),
                    in_=k_sb[b][:].rearrange("p u (c i) -> p c u i", i=4),
                )
            else:
                nc.gpsimd.tensor_scalar(
                    out=kg[:].rearrange("p (d u) -> p d u", u=PACK),
                    in0=k_sb[b][:].rearrange("p u d -> p d u"),
                    scalar1=1.0, scalar2=0.0, op0=ALU.mult, op1=ALU.add,
                )
            if b % 2 == 0:
                k_codes[b // 2] = (
                    resid.tile([P, 2 * D], U32, name="kc%d" % b, align_bytes=64),
                    resid.tile([P, 2 * D], U8, name="ks%d" % b, align_bytes=64),
                )
            codes, scales = k_codes[b // 2]
            c = slice((b % 2) * D, (b % 2 + 1) * D)
            nc.vector.quantize_mx(out=codes[:, c].bitcast(FP8X4), scales=scales[:, c], in_=kg[:])

        ALL = list(range(NB))

        def row_sums(b, blocks):
            if b not in state:
                state[b] = {
                    "deg": small.tile([P, NB], F32, name="deg"),
                    "sd": small.tile([P, NB], F32, name="sd"),
                    "thr": small.tile([P, NB], F32, name="thr"),
                }
            s = state[b]
            for i in blocks:
                unused = work.tile([P, T], BF16, name="unused")
                nc.scalar.activation(
                    out=unused[:], in_=rows(b)[:, i, :], func=ACT.Copy, accum_out=s["deg"][:, i : i + 1]
                )
            c = slice(blocks[0], blocks[-1] + 1)
            nc.scalar.activation(out=s["sd"][:, c], in_=s["deg"][:, c], func=ACT.Sqrt, bias=EPS)
            nc.scalar.mul(out=s["thr"][:, c], in_=s["sd"][:, c], mul=REL_THRESH)

        def scales(b, blocks):
            s = state[b]
            if "dis" not in s:
                s["dis"] = small.tile([P, NB], F32, name="dis")
            c = slice(blocks[0], blocks[-1] + 1)
            nc.vector.reciprocal(out=s["dis"][:, c], in_=s["sd"][:, c])

        def mask_and_abs(b, blocks):
            s = state[b]
            if "abs" not in s:
                s["abs"] = work.tile([P, NB * T], BF16, name="a_abs")
            a_words = a_sb[b][:, 0 : NB * T].bitcast(I32)
            abs_words = s["abs"][:].bitcast(I32)
            if len(blocks) == 1:
                i = blocks[0]
                n = (i + 1) * P
                diag = rows(b)[:, i, i * P : n]
                nc.vector.tensor_tensor(out=diag, in0=diag, in1=tril[:], op=ALU.mult)
                w0 = i * (T // 2)
                nc.vector.tensor_single_scalar(
                    out=abs_words[:, w0 : w0 + n // 2], in_=a_words[:, w0 : w0 + n // 2],
                    scalar=0x7FFF7FFF, op=ALU.bitwise_and,
                )
            else:
                diag = a_sb[b][:].rearrange("p (i x) -> p i x", x=DIAG_STEP)[:, :, 0:P]
                nc.vector.tensor_tensor(
                    out=diag, in0=diag, in1=tril[:].unsqueeze(1).to_broadcast([P, NB, P]), op=ALU.mult
                )
                nc.vector.tensor_single_scalar(out=abs_words, in_=a_words, scalar=0x7FFF7FFF, op=ALU.bitwise_and)

        def spread(b, blocks):
            s = state[b]
            if "dis_all" not in s:
                s["dis_all"] = ps_dis.tile([P, T], F32, name="dis_all")
                s["thr_all"] = ps_thr.tile([P, T], F32, name="thr_all")
            for dst, src in ((s["dis_all"], s["dis"]), (s["thr_all"], s["thr"])):
                for i in blocks:
                    nc.tensor.transpose(
                        out=dst[:, i * P : (i + 1) * P],
                        in_=src[:, i : i + 1].to_broadcast([P, P]),
                        identity=ident_f[:],
                    )

        def weights(b, i):
            s = state[b]
            if "w" not in s:
                s["w"] = work.tile([P, NB, T], BF16, name="w")
                wt_a = ps_wt.tile([P, 8, P], BF16, name="wt_a", bufs=2)
                wt_b = ps_wt.tile([P, 2, P], BF16, name="wt_b", bufs=1)
                s["wt"] = {3: (wt_a, 0), 2: (wt_a, 4), 0: (wt_a, 7), 1: (wt_b, 0)}
            n = (i + 1) * P
            nc.vector.scalar_tensor_tensor(
                out=s["w"][:, i, 0:n], in0=rows(b)[:, i, 0:n], scalar=s["dis"][:, i : i + 1],
                in1=s["dis_all"][:, 0:n], op0=ALU.mult, op1=ALU.mult,
            )
            wt, first = s["wt"][i]
            for u in range(i + 1):
                nc.tensor.transpose(
                    out=wt[:, first + u, :], in_=s["w"][:, i, u * P : (u + 1) * P], identity=ident_b[:]
                )
            g = grouped[b % N_GROUPED][:].rearrange("p (i t u) -> p i t u", t=P, u=PACK)
            nc.scalar.copy(
                out=g[:, i, :, 0 : i + 1], in_=wt[:, first : first + i + 1, :].rearrange("p u t -> p t u")
            )

        def count(b, i):
            s = state[b]
            if "cnt" not in s:
                s["cnt"] = small.tile([P, NB], F32, name="cnt")
            n = (i + 1) * P
            hits = work.tile([P, T], BF16, name="hits")
            nc.vector.scalar_tensor_tensor(
                out=hits[:, 0:n], in0=s["abs"][:].rearrange("p (i s) -> p i s", s=T)[:, i, 0:n],
                scalar=s["dis"][:, i : i + 1], in1=s["thr_all"][:, 0:n],
                op0=ALU.mult, op1=ALU.is_gt, accum_out=s["cnt"][:, i : i + 1],
            )

        def factor(b):
            s = state[b]
            s["fac"] = small.tile([P, NB], F32, name="fac")
            engine = nc.vector if b == B - 1 else nc.gpsimd
            engine.tensor_scalar(
                out=s["fac"][:], in0=s["cnt"][:], scalar1=0.5, scalar2=math.sqrt(GAMMA),
                op0=ALU.is_gt, op1=ALU.mult,
            )

        def product(b):
            s = state[b]
            g = grouped[b % N_GROUPED]
            kc, ks = k_codes[b // 2]
            mine = slice((b % 2) * D, (b % 2 + 1) * D)
            last = b == B - 1
            codes = work.tile([P, NB * P], U32, name="wc", align_bytes=64)
            scl = work.tile([P, NB * P], U8, name="ws", align_bytes=64)
            res = work.tile([P, NB, D], F32, name="res")
            dst = out[b].rearrange("(i p) d -> p i d", p=P)
            if not last:
                nc.vector.quantize_mx(out=codes[:].bitcast(FP8X4), scales=scl[:], in_=g[:])
            for h in (1, 0):
                if last:
                    c = slice(h * 2 * P, (h + 1) * 2 * P)
                    nc.vector.quantize_mx(
                        out=codes[:, c].bitcast(FP8X4), scales=scl[:, c],
                        in_=g[:, h * 2 * P * PACK : (h + 1) * 2 * P * PACK],
                    )
                accs = []
                for j in range(2):
                    c = slice((2 * h + j) * P, (2 * h + j + 1) * P)
                    acc = ps_out.tile([P, 2 * D], F32, name="acc")
                    accs.append(acc)
                    nc.tensor.matmul_mx(
                        out=acc[:],
                        lhsT=codes[:, c].bitcast(FP8X4), lhsT_scale=scl[:, c],
                        rhs=kc[:].bitcast(FP8X4), rhs_scale=ks[:],
                        start=True, stop=True,
                    )
                for j in range(2):
                    i = 2 * h + j
                    if last and j == 1:
                        nc.vector.tensor_scalar_mul(out=res[:, i, :], in0=accs[j][:, mine], scalar1=s["fac"][:, i : i + 1])
                    else:
                        nc.scalar.activation(
                            out=res[:, i, :], in_=accs[j][:, mine], func=ACT.Copy, scale=s["fac"][:, i : i + 1]
                        )
                if last:
                    nc.sync.dma_start(out=dst[:, 2 * h : 2 * h + 2, :], in_=res[:, 2 * h : 2 * h + 2, :])
            if not last:
                nc.sync.dma_start(out=dst, in_=res[:])

        for i in ALL:
            row_sums(0, [i])
            scales(0, [i])
            mask_and_abs(0, [i])
            spread(0, [i])
            weights(0, i)
            count(0, i)
        factor(0)
        for b in range(K_ON_VECTOR):
            prepare_k(b)
        for b in range(1, B + 2):
            if b < B:
                row_sums(b, ALL)
                scales(b, ALL)
                mask_and_abs(b, ALL)
                spread(b, ALL)
                if b >= K_ON_VECTOR:
                    prepare_k(b)
            if 1 <= b - 1 < B:
                for i in reversed(ALL):
                    weights(b - 1, i)
                for i in reversed(ALL):
                    count(b - 1, i)
                factor(b - 1)
            if b - 2 >= 0:
                product(b - 2)
